import numpy as np
import ml_dtypes

BF16 = ml_dtypes.bfloat16


def bf(x):
    return np.asarray(x, np.float32).astype(BF16)


def f32(x):
    return np.asarray(x, np.float32)


def f64(x):
    return np.asarray(x).astype(np.float64)


def striped(idx):
    return np.tile(idx.reshape(-1, 16).T, (8, 1))


C, S, N, T, F = 512, 4096, 512, 4, 512


def pos_encoding():
    t = np.tile(np.arange(T, dtype=np.float64), N // T)
    pe = np.zeros((C, N))
    pe[0] = t
    pe[1] = 1.0 / np.log(2.0) - 1.0 / np.log(t + 2.0)
    pe[2] = t * t
    return pe


def setup_inputs():
    return {"tok_emb": f32(np.random.standard_normal((C, S))), "pos_enc": f32(pos_encoding()), "w_in": bf(np.random.standard_normal((C, 2 * F)) / np.sqrt(C)), "w_out": bf(np.random.standard_normal((F, C)) / np.sqrt(F)), "offs": striped(np.random.permutation(np.tile(np.arange(S), 2))[:N])}


def reference(tok_emb, pos_enc, w_in, w_out, offs):
    idx = offs[:16].T.reshape(-1)
    x = f64(tok_emb)[:, idx] + f64(pos_enc)
    gv = f64(w_in).T @ x
    h = np.maximum(gv[:F], 0.0) * gv[F:]
    return x + f64(w_out).T @ h

@@ -1,0 +1,73 @@
+import concourse.mybir as mybir
+
+F32 = mybir.dt.float32
+BF16 = mybir.dt.bfloat16
+U16 = mybir.dt.uint16
+ADD = mybir.AluOpType.add
+MULT = mybir.AluOpType.mult
+COPY = mybir.ActivationFunctionType.Copy
+RELU = mybir.ActivationFunctionType.Relu
+
+P = 128
+C, S, N, F = 512, 4096, 512, 512
+CB = C // P
+FB = F // P
+
+FLOPS = 2 * C * (2 * F) * N + 2 * F * C * N
+
+
+def tile_vanillatransformer_kernel(tc, tok_emb, pos_enc, w_in, w_out, offs, out):
+    nc = tc.nc
+    with (
+        tc.tile_pool(name="held", bufs=1) as held,
+        tc.tile_pool(name="work", bufs=2) as work,
+        tc.psum_pool(name="psum", bufs=8) as psum,
+    ):
+        offsets = held.tile([P, N // 16], U16, name="offsets")
+        nc.sync.dma_start(offsets[:], offs)
+
+        table = [held.tile([P, S], F32, name=f"table{k}") for k in range(CB)]
+        pos = [held.tile([P, N], F32, name=f"pos{k}") for k in range(CB)]
+        w_in_sb = [held.tile([P, 2 * F], BF16, name=f"w_in_sb{k}") for k in range(CB)]
+        w_out_sb = held.tile([P, FB, C], BF16, name="w_out_sb")
+        for k in range(CB):
+            rows = slice(k * P, (k + 1) * P)
+            nc.sync.dma_start(pos[k][:], pos_enc[rows, :])
+            nc.sync.dma_start(table[k][:], tok_emb[rows, :])
+            nc.sync.dma_start(w_in_sb[k][:], w_in[rows, :])
+        nc.sync.dma_start(w_out_sb[:], w_out.rearrange("(f p) c -> p f c", p=P))
+
+        gate = []
+        val = []
+        for f in range(FB):
+            gate.append(psum.tile([P, N], F32, name=f"gate{f}", tag="bank"))
+            val.append(psum.tile([P, N], F32, name=f"val{f}", tag="bank"))
+        x32 = [held.tile([P, N], F32, name=f"x32_{k}") for k in range(CB)]
+        x16 = [held.tile([P, N], BF16, name=f"x16_{k}") for k in range(CB)]
+        for k in range(CB):
+            nc.vector.tensor_tensor(x32[k][:], table[k][:].indirect(offsets[:]), pos[k][:], ADD)
+            nc.scalar.activation(x16[k][:], x32[k][:], COPY)
+            first, last = k == 0, k == CB - 1
+            for f in range(FB):
+                nc.tensor.matmul(
+                    gate[f][:], w_in_sb[k][:, f * P : (f + 1) * P], x16[k][:], start=first, stop=last
+                )
+                nc.tensor.matmul(
+                    val[f][:], w_in_sb[k][:, F + f * P : F + (f + 1) * P], x16[k][:], start=first, stop=last
+                )
+
+        h = [held.tile([P, N], BF16, name=f"h{f}") for f in range(FB)]
+        for f in range(FB):
+            relu_gate = work.tile([P, N], F32, name="relu_gate")
+            nc.scalar.activation(relu_gate[:], gate[f][:], RELU)
+            nc.vector.tensor_tensor(h[f][:], relu_gate[:], val[f][:], MULT)
+
+        for m in range(CB):
+            ffn = psum.tile([P, N], F32, name="ffn", tag="bank")
+            for f in range(FB):
+                nc.tensor.matmul(
+                    ffn[:], w_out_sb[:, f, m * P : (m + 1) * P], h[f][:], start=f == 0, stop=f == FB - 1
+                )
+            result = work.tile([P, N], F32, name="result")
+            nc.vector.tensor_tensor(result[:], ffn[:], x32[m][:], ADD)
+            nc.sync.dma_start(out[m * P : (m + 1) * P, :], result[:])

@@ -12,6 +12,9 @@ P = 128
 C, S, N, F = 512, 4096, 512, 512
 CB = C // P
 FB = F // P
+PW = 128
+NP = N // PW
+OC = PW // 16
 
 FLOPS = 2 * C * (2 * F) * N + 2 * F * C * N
 
@@ -20,7 +23,7 @@ def tile_vanillatransformer_kernel(tc, tok_emb, pos_enc, w_in, w_out, offs, out)
     nc = tc.nc
     with (
         tc.tile_pool(name="held", bufs=1) as held,
-        tc.tile_pool(name="work", bufs=2) as work,
+        tc.tile_pool(name="work", bufs=4) as work,
         tc.psum_pool(name="psum", bufs=8) as psum,
     ):
         offsets = held.tile([P, N // 16], U16, name="offsets")
@@ -37,37 +40,52 @@ def tile_vanillatransformer_kernel(tc, tok_emb, pos_enc, w_in, w_out, offs, out)
             nc.sync.dma_start(w_in_sb[k][:], w_in[rows, :])
         nc.sync.dma_start(w_out_sb[:], w_out.rearrange("(f p) c -> p f c", p=P))
 
-        gate = []
-        val = []
-        for f in range(FB):
-            gate.append(psum.tile([P, N], F32, name=f"gate{f}", tag="bank"))
-            val.append(psum.tile([P, N], F32, name=f"val{f}", tag="bank"))
-        x32 = [held.tile([P, N], F32, name=f"x32_{k}") for k in range(CB)]
-        x16 = [held.tile([P, N], BF16, name=f"x16_{k}") for k in range(CB)]
+        gate = [psum.tile([P, FB, PW], F32, name=f"gate{p}", tag="bank") for p in range(NP)]
+        val = [psum.tile([P, FB, PW], F32, name=f"val{p}", tag="bank") for p in range(NP)]
+        x32 = [held.tile([P, CB, PW], F32, name=f"x32_{p}") for p in range(NP)]
+        x16 = [held.tile([P, CB, PW], BF16, name=f"x16_{p}") for p in range(NP)]
+        h = [held.tile([P, FB, PW], BF16, name=f"h{p}") for p in range(NP)]
+
         for k in range(CB):
-            nc.vector.tensor_tensor(x32[k][:], table[k][:].indirect(offsets[:]), pos[k][:], ADD)
-            nc.scalar.activation(x16[k][:], x32[k][:], COPY)
-            first, last = k == 0, k == CB - 1
-            for f in range(FB):
-                nc.tensor.matmul(
-                    gate[f][:], w_in_sb[k][:, f * P : (f + 1) * P], x16[k][:], start=first, stop=last
+            for p in range(NP):
+                nc.vector.tensor_tensor(
+                    x32[p][:, k, :],
+                    table[k][:].indirect(offsets[:, p * OC : (p + 1) * OC]),
+                    pos[k][:, p * PW : (p + 1) * PW],
+                    ADD,
                 )
-                nc.tensor.matmul(
-                    val[f][:], w_in_sb[k][:, F + f * P : F + (f + 1) * P], x16[k][:], start=first, stop=last
-                )
+                nc.scalar.activation(x16[p][:, k, :], x32[p][:, k, :], COPY)
+                for f in range(FB):
+                    first = k == 0 and f == 0
+                    last = k == CB - 1 and f == FB - 1
+                    nc.tensor.matmul(
+                        gate[p][:, f, :], w_in_sb[k][:, f * P : (f + 1) * P], x16[p][:, k, :], start=first, stop=last
+                    )
+                    nc.tensor.matmul(
+                        val[p][:, f, :],
+                        w_in_sb[k][:, F + f * P : F + (f + 1) * P],
+                        x16[p][:, k, :],
+                        start=first,
+                        stop=last,
+                    )
 
-        h = [held.tile([P, N], BF16, name=f"h{f}") for f in range(FB)]
-        for f in range(FB):
-            relu_gate = work.tile([P, N], F32, name="relu_gate")
-            nc.scalar.activation(relu_gate[:], gate[f][:], RELU)
-            nc.vector.tensor_tensor(h[f][:], relu_gate[:], val[f][:], MULT)
+        for p in range(NP):
+            relu_gate = work.tile([P, FB, PW], F32, name="relu_gate")
+            nc.scalar.activation(relu_gate[:], gate[p][:], RELU)
+            nc.vector.tensor_tensor(h[p][:], relu_gate[:], val[p][:], MULT)
 
-        for m in range(CB):
-            ffn = psum.tile([P, N], F32, name="ffn", tag="bank")
-            for f in range(FB):
-                nc.tensor.matmul(
-                    ffn[:], w_out_sb[:, f, m * P : (m + 1) * P], h[f][:], start=f == 0, stop=f == FB - 1
-                )
-            result = work.tile([P, N], F32, name="result")
-            nc.vector.tensor_tensor(result[:], ffn[:], x32[m][:], ADD)
-            nc.sync.dma_start(out[m * P : (m + 1) * P, :], result[:])
+        out_blocks = out.rearrange("(m q) j -> q m j", q=P)
+        for p in range(NP):
+            ffn = psum.tile([P, CB, PW], F32, name="ffn", tag="bank")
+            for m in range(CB):
+                for f in range(FB):
+                    nc.tensor.matmul(
+                        ffn[:, m, :],
+                        w_out_sb[:, f, m * P : (m + 1) * P],
+                        h[p][:, f, :],
+                        start=m == 0 and f == 0,
+                        stop=m == CB - 1 and f == FB - 1,
+                    )
+            result = work.tile([P, CB, PW], F32, name="result")
+            nc.vector.tensor_tensor(result[:], ffn[:], x32[p][:], ADD)
+            nc.sync.dma_start(out_blocks[:, :, p * PW : (p + 1) * PW], result[:])

@@ -36,8 +36,9 @@ def tile_vanillatransformer_kernel(tc, tok_emb, pos_enc, w_in, w_out, offs, out)
         for k in range(CB):
             rows = slice(k * P, (k + 1) * P)
             nc.sync.dma_start(pos[k][:], pos_enc[rows, :])
-            nc.sync.dma_start(table[k][:], tok_emb[rows, :])
-            nc.sync.dma_start(w_in_sb[k][:], w_in[rows, :])
+            nc.sync.dma_start(table[k][:, : S // 2], tok_emb[rows, : S // 2])
+            nc.scalar.dma_start(table[k][:, S // 2 :], tok_emb[rows, S // 2 :])
+            nc.scalar.dma_start(w_in_sb[k][:], w_in[rows, :])
         nc.sync.dma_start(w_out_sb[:], w_out.rearrange("(f p) c -> p f c", p=P))
 
         gate = [psum.tile([P, FB, PW], F32, name=f"gate{p}", tag="bank") for p in range(NP)]

@@ -5,7 +5,6 @@ BF16 = mybir.dt.bfloat16
 U16 = mybir.dt.uint16
 ADD = mybir.AluOpType.add
 MULT = mybir.AluOpType.mult
-COPY = mybir.ActivationFunctionType.Copy
 RELU = mybir.ActivationFunctionType.Relu
 
 P = 128
@@ -36,9 +35,8 @@ def tile_vanillatransformer_kernel(tc, tok_emb, pos_enc, w_in, w_out, offs, out)
         for k in range(CB):
             rows = slice(k * P, (k + 1) * P)
             nc.sync.dma_start(pos[k][:], pos_enc[rows, :])
-            nc.sync.dma_start(table[k][:, : S // 2], tok_emb[rows, : S // 2])
-            nc.scalar.dma_start(table[k][:, S // 2 :], tok_emb[rows, S // 2 :])
-            nc.scalar.dma_start(w_in_sb[k][:], w_in[rows, :])
+            nc.sync.dma_start(table[k][:], tok_emb[rows, :])
+            nc.sync.dma_start(w_in_sb[k][:], w_in[rows, :])
         nc.sync.dma_start(w_out_sb[:], w_out.rearrange("(f p) c -> p f c", p=P))
 
         gate = [psum.tile([P, FB, PW], F32, name=f"gate{p}", tag="bank") for p in range(NP)]
@@ -55,7 +53,7 @@ def tile_vanillatransformer_kernel(tc, tok_emb, pos_enc, w_in, w_out, offs, out)
                     pos[k][:, p * PW : (p + 1) * PW],
                     ADD,
                 )
-                nc.scalar.activation(x16[p][:, k, :], x32[p][:, k, :], COPY)
+                nc.vector.tensor_copy(x16[p][:, k, :], x32[p][:, k, :])
                 for f in range(FB):
                     first = k == 0 and f == 0
                     last = k == CB - 1 and f == FB - 1

@@ -5,6 +5,7 @@ BF16 = mybir.dt.bfloat16
 U16 = mybir.dt.uint16
 ADD = mybir.AluOpType.add
 MULT = mybir.AluOpType.mult
+COPY = mybir.ActivationFunctionType.Copy
 RELU = mybir.ActivationFunctionType.Relu
 
 P = 128
@@ -35,8 +36,14 @@ def tile_vanillatransformer_kernel(tc, tok_emb, pos_enc, w_in, w_out, offs, out)
         for k in range(CB):
             rows = slice(k * P, (k + 1) * P)
             nc.sync.dma_start(pos[k][:], pos_enc[rows, :])
-            nc.sync.dma_start(table[k][:], tok_emb[rows, :])
-            nc.sync.dma_start(w_in_sb[k][:], w_in[rows, :])
+            if k == CB - 2:
+                nc.sync.dma_start(table[k][:, : S // 2], tok_emb[rows, : S // 2])
+                for kk in range(CB - 1):
+                    nc.sync.dma_start(w_in_sb[kk][:], w_in[kk * P : (kk + 1) * P, :])
+                nc.sync.dma_start(table[k][:, S // 2 :], tok_emb[rows, S // 2 :])
+            else:
+                nc.sync.dma_start(table[k][:], tok_emb[rows, :])
+        nc.sync.dma_start(w_in_sb[CB - 1][:], w_in[(CB - 1) * P :, :])
         nc.sync.dma_start(w_out_sb[:], w_out.rearrange("(f p) c -> p f c", p=P))
 
         gate = [psum.tile([P, FB, PW], F32, name=f"gate{p}", tag="bank") for p in range(NP)]
@@ -53,7 +60,7 @@ def tile_vanillatransformer_kernel(tc, tok_emb, pos_enc, w_in, w_out, offs, out)
                     pos[k][:, p * PW : (p + 1) * PW],
                     ADD,
                 )
-                nc.vector.tensor_copy(x16[p][:, k, :], x32[p][:, k, :])
+                nc.scalar.activation(x16[p][:, k, :], x32[p][:, k, :], COPY)
                 for f in range(FB):
                     first = k == 0 and f == 0
                     last = k == CB - 1 and f == FB - 1

@@ -12,9 +12,6 @@ P = 128
 C, S, N, F = 512, 4096, 512, 512
 CB = C // P
 FB = F // P
-PW = 128
-NP = N // PW
-OC = PW // 16
 
 FLOPS = 2 * C * (2 * F) * N + 2 * F * C * N
 
@@ -23,7 +20,7 @@ def tile_vanillatransformer_kernel(tc, tok_emb, pos_enc, w_in, w_out, offs, out)
     nc = tc.nc
     with (
         tc.tile_pool(name="held", bufs=1) as held,
-        tc.tile_pool(name="work", bufs=4) as work,
+        tc.tile_pool(name="work", bufs=2) as work,
         tc.psum_pool(name="psum", bufs=8) as psum,
     ):
         offsets = held.tile([P, N // 16], U16, name="offsets")
@@ -36,62 +33,43 @@ def tile_vanillatransformer_kernel(tc, tok_emb, pos_enc, w_in, w_out, offs, out)
         for k in range(CB):
             rows = slice(k * P, (k + 1) * P)
             nc.sync.dma_start(pos[k][:], pos_enc[rows, :])
-            if k == CB - 2:
-                nc.sync.dma_start(table[k][:, : S // 2], tok_emb[rows, : S // 2])
-                for kk in range(CB - 1):
-                    nc.sync.dma_start(w_in_sb[kk][:], w_in[kk * P : (kk + 1) * P, :])
-                nc.sync.dma_start(table[k][:, S // 2 :], tok_emb[rows, S // 2 :])
-            else:
-                nc.sync.dma_start(table[k][:], tok_emb[rows, :])
-        nc.sync.dma_start(w_in_sb[CB - 1][:], w_in[(CB - 1) * P :, :])
+            nc.sync.dma_start(table[k][:], tok_emb[rows, :])
+            nc.sync.dma_start(w_in_sb[k][:], w_in[rows, :])
         nc.sync.dma_start(w_out_sb[:], w_out.rearrange("(f p) c -> p f c", p=P))
 
-        gate = [psum.tile([P, FB, PW], F32, name=f"gate{p}", tag="bank") for p in range(NP)]
-        val = [psum.tile([P, FB, PW], F32, name=f"val{p}", tag="bank") for p in range(NP)]
-        x32 = [held.tile([P, CB, PW], F32, name=f"x32_{p}") for p in range(NP)]
-        x16 = [held.tile([P, CB, PW], BF16, name=f"x16_{p}") for p in range(NP)]
-        h = [held.tile([P, FB, PW], BF16, name=f"h{p}") for p in range(NP)]
-
+        gate = []
+        val = []
+        for f in range(FB):
+            gate.append(psum.tile([P, N], F32, name=f"gate{f}", tag="bank"))
+            val.append(psum.tile([P, N], F32, name=f"val{f}", tag="bank"))
+        x32 = [held.tile([P, N], F32, name=f"x32_{k}") for k in range(CB)]
+        x16 = [held.tile([P, N], BF16, name=f"x16_{k}") for k in range(CB)]
         for k in range(CB):
-            for p in range(NP):
-                nc.vector.tensor_tensor(
-                    x32[p][:, k, :],
-                    table[k][:].indirect(offsets[:, p * OC : (p + 1) * OC]),
-                    pos[k][:, p * PW : (p + 1) * PW],
-                    ADD,
+            nc.vector.tensor_tensor(x32[k][:], table[k][:].indirect(offsets[:]), pos[k][:], ADD)
+            nc.scalar.activation(x16[k][:], x32[k][:], COPY)
+            first, last = k == 0, k == CB - 1
+            for f in range(FB):
+                nc.tensor.matmul(
+                    gate[f][:], w_in_sb[k][:, f * P : (f + 1) * P], x16[k][:], start=first, stop=last
                 )
-                nc.scalar.activation(x16[p][:, k, :], x32[p][:, k, :], COPY)
-                for f in range(FB):
-                    first = k == 0 and f == 0
-                    last = k == CB - 1 and f == FB - 1
-                    nc.tensor.matmul(
-                        gate[p][:, f, :], w_in_sb[k][:, f * P : (f + 1) * P], x16[p][:, k, :], start=first, stop=last
-                    )
-                    nc.tensor.matmul(
-                        val[p][:, f, :],
-                        w_in_sb[k][:, F + f * P : F + (f + 1) * P],
-                        x16[p][:, k, :],
-                        start=first,
-                        stop=last,
-                    )
+                nc.tensor.matmul(
+                    val[f][:], w_in_sb[k][:, F + f * P : F + (f + 1) * P], x16[k][:], start=first, stop=last
+                )
 
-        for p in range(NP):
-            relu_gate = work.tile([P, FB, PW], F32, name="relu_gate")
-            nc.scalar.activation(relu_gate[:], gate[p][:], RELU)
-            nc.vector.tensor_tensor(h[p][:], relu_gate[:], val[p][:], MULT)
+        h = [held.tile([P, N], BF16, name=f"h{f}") for f in range(FB)]
+        for f in range(FB):
+            relu_gate = work.tile([P, N], F32, name="relu_gate")
+            nc.scalar.activation(relu_gate[:], gate[f][:], RELU)
+            nc.vector.tensor_tensor(h[f][:], relu_gate[:], val[f][:], MULT)
 
-        out_blocks = out.rearrange("(m q) j -> q m j", q=P)
-        for p in range(NP):
-            ffn = psum.tile([P, CB, PW], F32, name="ffn", tag="bank")
-            for m in range(CB):
-                for f in range(FB):
+        for group in ((0, 1), (2,), (3,)):
+            ffn = {m: psum.tile([P, N], F32, name=f"ffn{m}", tag="bank") for m in group}
+            for f in range(FB):
+                for m in group:
                     nc.tensor.matmul(
-                        ffn[:, m, :],
-                        w_out_sb[:, f, m * P : (m + 1) * P],
-                        h[p][:, f, :],
-                        start=m == 0 and f == 0,
-                        stop=m == CB - 1 and f == FB - 1,
+                        ffn[m][:], w_out_sb[:, f, m * P : (m + 1) * P], h[f][:], start=f == 0, stop=f == FB - 1
                     )
-            result = work.tile([P, CB, PW], F32, name="result")
-            nc.vector.tensor_tensor(result[:], ffn[:], x32[p][:], ADD)
-            nc.sync.dma_start(out_blocks[:, :, p * PW : (p + 1) * PW], result[:])
+            for m in group:
+                result = work.tile([P, N], F32, name="result")
+                nc.vector.tensor_tensor(result[:], ffn[m][:], x32[m][:], ADD)
+                nc.sync.dma_start(out[m * P : (m + 1) * P, :], result[:])

@@ -20,7 +20,7 @@ def tile_vanillatransformer_kernel(tc, tok_emb, pos_enc, w_in, w_out, offs, out)
     nc = tc.nc
     with (
         tc.tile_pool(name="held", bufs=1) as held,
-        tc.tile_pool(name="work", bufs=2) as work,
+        tc.tile_pool(name="work", bufs=4) as work,
         tc.psum_pool(name="psum", bufs=8) as psum,
     ):
         offsets = held.tile([P, N // 16], U16, name="offsets")
@@ -62,14 +62,12 @@ def tile_vanillatransformer_kernel(tc, tok_emb, pos_enc, w_in, w_out, offs, out)
             nc.scalar.activation(relu_gate[:], gate[f][:], RELU)
             nc.vector.tensor_tensor(h[f][:], relu_gate[:], val[f][:], MULT)
 
-        for group in ((0, 1), (2,), (3,)):
-            ffn = {m: psum.tile([P, N], F32, name=f"ffn{m}", tag="bank") for m in group}
+        for m in range(CB):
+            ffn = psum.tile([P, N], F32, name="ffn", tag="bank")
             for f in range(FB):
-                for m in group:
-                    nc.tensor.matmul(
-                        ffn[m][:], w_out_sb[:, f, m * P : (m + 1) * P], h[f][:], start=f == 0, stop=f == FB - 1
-                    )
-            for m in group:
-                result = work.tile([P, N], F32, name="result")
-                nc.vector.tensor_tensor(result[:], ffn[m][:], x32[m][:], ADD)
-                nc.sync.dma_start(out[m * P : (m + 1) * P, :], result[:])
+                nc.tensor.matmul(
+                    ffn[:], w_out_sb[:, f, m * P : (m + 1) * P], h[f][:], start=f == 0, stop=f == FB - 1
+                )
+            result = work.tile([P, N], F32, name="result")
+            nc.vector.tensor_tensor(result[:], ffn[:], x32[m][:], ADD)
+            nc.sync.dma_start(out[m * P : (m + 1) * P, :], result[:])

@@ -12,6 +12,7 @@ P = 128
 C, S, N, F = 512, 4096, 512, 512
 CB = C // P
 FB = F // P
+BANKS = 8
 
 FLOPS = 2 * C * (2 * F) * N + 2 * F * C * N
 
@@ -21,20 +22,26 @@ def tile_vanillatransformer_kernel(tc, tok_emb, pos_enc, w_in, w_out, offs, out)
     with (
         tc.tile_pool(name="held", bufs=1) as held,
         tc.tile_pool(name="work", bufs=4) as work,
-        tc.psum_pool(name="psum", bufs=8) as psum,
+        tc.psum_pool(name="psum", bufs=BANKS) as psum,
     ):
         offsets = held.tile([P, N // 16], U16, name="offsets")
-        nc.sync.dma_start(offsets[:], offs)
-
         table = [held.tile([P, S], F32, name=f"table{k}") for k in range(CB)]
         pos = [held.tile([P, N], F32, name=f"pos{k}") for k in range(CB)]
         w_in_sb = [held.tile([P, 2 * F], BF16, name=f"w_in_sb{k}") for k in range(CB)]
         w_out_sb = held.tile([P, FB, C], BF16, name="w_out_sb")
-        for k in range(CB):
-            rows = slice(k * P, (k + 1) * P)
-            nc.sync.dma_start(pos[k][:], pos_enc[rows, :])
-            nc.sync.dma_start(table[k][:], tok_emb[rows, :])
-            nc.sync.dma_start(w_in_sb[k][:], w_in[rows, :])
+        x32 = [held.tile([P, N], F32, name=f"x32_{k}") for k in range(CB)]
+        x16 = [held.tile([P, N], BF16, name=f"x16_{k}") for k in range(CB)]
+        h = [held.tile([P, N], BF16, name=f"h{f}") for f in range(FB)]
+
+        nc.sync.dma_start(offsets[:], offs)
+        for k in range(CB - 1):
+            nc.sync.dma_start(pos[k][:], pos_enc[k * P : (k + 1) * P, :])
+            nc.sync.dma_start(table[k][:], tok_emb[k * P : (k + 1) * P, :])
+        for k in range(CB - 1):
+            nc.sync.dma_start(w_in_sb[k][:], w_in[k * P : (k + 1) * P, :])
+        nc.sync.dma_start(pos[CB - 1][:], pos_enc[(CB - 1) * P :, :])
+        nc.sync.dma_start(table[CB - 1][:], tok_emb[(CB - 1) * P :, :])
+        nc.sync.dma_start(w_in_sb[CB - 1][:], w_in[(CB - 1) * P :, :])
         nc.sync.dma_start(w_out_sb[:], w_out.rearrange("(f p) c -> p f c", p=P))
 
         gate = []
@@ -42,21 +49,17 @@ def tile_vanillatransformer_kernel(tc, tok_emb, pos_enc, w_in, w_out, offs, out)
         for f in range(FB):
             gate.append(psum.tile([P, N], F32, name=f"gate{f}", tag="bank"))
             val.append(psum.tile([P, N], F32, name=f"val{f}", tag="bank"))
-        x32 = [held.tile([P, N], F32, name=f"x32_{k}") for k in range(CB)]
-        x16 = [held.tile([P, N], BF16, name=f"x16_{k}") for k in range(CB)]
         for k in range(CB):
             nc.vector.tensor_tensor(x32[k][:], table[k][:].indirect(offsets[:]), pos[k][:], ADD)
             nc.scalar.activation(x16[k][:], x32[k][:], COPY)
-            first, last = k == 0, k == CB - 1
             for f in range(FB):
                 nc.tensor.matmul(
-                    gate[f][:], w_in_sb[k][:, f * P : (f + 1) * P], x16[k][:], start=first, stop=last
+                    gate[f][:], w_in_sb[k][:, f * P : (f + 1) * P], x16[k][:], start=k == 0, stop=k == CB - 1
                 )
                 nc.tensor.matmul(
-                    val[f][:], w_in_sb[k][:, F + f * P : F + (f + 1) * P], x16[k][:], start=first, stop=last
+                    val[f][:], w_in_sb[k][:, F + f * P : F + (f + 1) * P], x16[k][:], start=k == 0, stop=k == CB - 1
                 )
 
-        h = [held.tile([P, N], BF16, name=f"h{f}") for f in range(FB)]
         for f in range(FB):
             relu_gate = work.tile([P, N], F32, name="relu_gate")
             nc.scalar.activation(relu_gate[:], gate[f][:], RELU)

@@ -13,6 +13,7 @@ C, S, N, F = 512, 4096, 512, 512
 CB = C // P
 FB = F // P
 BANKS = 8
+LAST_CUTS = 4
 
 FLOPS = 2 * C * (2 * F) * N + 2 * F * C * N
 
@@ -50,27 +51,44 @@ def tile_vanillatransformer_kernel(tc, tok_emb, pos_enc, w_in, w_out, offs, out)
             gate.append(psum.tile([P, N], F32, name=f"gate{f}", tag="bank"))
             val.append(psum.tile([P, N], F32, name=f"val{f}", tag="bank"))
         for k in range(CB):
-            nc.vector.tensor_tensor(x32[k][:], table[k][:].indirect(offsets[:]), pos[k][:], ADD)
-            nc.scalar.activation(x16[k][:], x32[k][:], COPY)
-            for f in range(FB):
-                nc.tensor.matmul(
-                    gate[f][:], w_in_sb[k][:, f * P : (f + 1) * P], x16[k][:], start=k == 0, stop=k == CB - 1
+            cuts = LAST_CUTS if k == CB - 1 else 1
+            width = N // cuts
+            for t in range(cuts):
+                cols = slice(t * width, (t + 1) * width)
+                nc.vector.tensor_tensor(
+                    x32[k][:, cols],
+                    table[k][:].indirect(offsets[:, t * width // 16 : (t + 1) * width // 16]),
+                    pos[k][:, cols],
+                    ADD,
                 )
-                nc.tensor.matmul(
-                    val[f][:], w_in_sb[k][:, F + f * P : F + (f + 1) * P], x16[k][:], start=k == 0, stop=k == CB - 1
-                )
+                nc.scalar.activation(x16[k][:, cols], x32[k][:, cols], COPY)
+                last = k == CB - 1 and t == cuts - 1
+                for f in range(FB):
+                    nc.tensor.matmul(
+                        gate[f][:, cols], w_in_sb[k][:, f * P : (f + 1) * P], x16[k][:, cols], start=k == 0, stop=last
+                    )
+                    nc.tensor.matmul(
+                        val[f][:, cols],
+                        w_in_sb[k][:, F + f * P : F + (f + 1) * P],
+                        x16[k][:, cols],
+                        start=k == 0,
+                        stop=last,
+                    )
 
         for f in range(FB):
             relu_gate = work.tile([P, N], F32, name="relu_gate")
             nc.scalar.activation(relu_gate[:], gate[f][:], RELU)
             nc.vector.tensor_tensor(h[f][:], relu_gate[:], val[f][:], MULT)
 
+        ffn = [psum.tile([P, N], F32, name=f"ffn{m}", tag="bank") for m in range(CB)]
+        for f in range(FB // 2):
+            for m in range(CB):
+                nc.tensor.matmul(ffn[m][:], w_out_sb[:, f, m * P : (m + 1) * P], h[f][:], start=f == 0, stop=False)
         for m in range(CB):
-            ffn = psum.tile([P, N], F32, name="ffn", tag="bank")
-            for f in range(FB):
+            for f in range(FB // 2, FB):
                 nc.tensor.matmul(
-                    ffn[:], w_out_sb[:, f, m * P : (m + 1) * P], h[f][:], start=f == 0, stop=f == FB - 1
+                    ffn[m][:], w_out_sb[:, f, m * P : (m + 1) * P], h[f][:], start=False, stop=f == FB - 1
                 )
             result = work.tile([P, N], F32, name="result")
-            nc.vector.tensor_tensor(result[:], ffn[:], x32[m][:], ADD)
+            nc.vector.tensor_tensor(result[:], ffn[m][:], x32[m][:], ADD)
             nc.sync.dma_start(out[m * P : (m + 1) * P, :], result[:])

@@ -62,18 +62,13 @@ def tile_vanillatransformer_kernel(tc, tok_emb, pos_enc, w_in, w_out, offs, out)
                     ADD,
                 )
                 nc.scalar.activation(x16[k][:, cols], x32[k][:, cols], COPY)
-                last = k == CB - 1 and t == cuts - 1
-                for f in range(FB):
-                    nc.tensor.matmul(
-                        gate[f][:, cols], w_in_sb[k][:, f * P : (f + 1) * P], x16[k][:, cols], start=k == 0, stop=last
-                    )
-                    nc.tensor.matmul(
-                        val[f][:, cols],
-                        w_in_sb[k][:, F + f * P : F + (f + 1) * P],
-                        x16[k][:, cols],
-                        start=k == 0,
-                        stop=last,
-                    )
+            for f in range(FB):
+                nc.tensor.matmul(
+                    gate[f][:], w_in_sb[k][:, f * P : (f + 1) * P], x16[k][:], start=k == 0, stop=k == CB - 1
+                )
+                nc.tensor.matmul(
+                    val[f][:], w_in_sb[k][:, F + f * P : F + (f + 1) * P], x16[k][:], start=k == 0, stop=k == CB - 1
+                )
 
         for f in range(FB):
             relu_gate = work.tile([P, N], F32, name="relu_gate")

@@ -20,6 +20,11 @@ FLOPS = 2 * C * (2 * F) * N + 2 * F * C * N
 
 def tile_vanillatransformer_kernel(tc, tok_emb, pos_enc, w_in, w_out, offs, out):
     nc = tc.nc
+    tok_blocks = tok_emb.rearrange("(p k) s -> k p s", k=CB)
+    out_blocks = out.rearrange("(p k) j -> k p j", k=CB)
+    pos_rows = pos_enc.rearrange("(p k) j -> p k j", k=CB)
+    w_in_rows = w_in.rearrange("(p k) f -> p k f", k=CB)
+    w_out_rows = w_out.rearrange("(f p) (q k) -> p f q k", p=P, k=CB)
     with (
         tc.tile_pool(name="held", bufs=1) as held,
         tc.tile_pool(name="work", bufs=4) as work,
@@ -27,23 +32,23 @@ def tile_vanillatransformer_kernel(tc, tok_emb, pos_enc, w_in, w_out, offs, out)
     ):
         offsets = held.tile([P, N // 16], U16, name="offsets")
         table = [held.tile([P, S], F32, name=f"table{k}") for k in range(CB)]
-        pos = [held.tile([P, N], F32, name=f"pos{k}") for k in range(CB)]
-        w_in_sb = [held.tile([P, 2 * F], BF16, name=f"w_in_sb{k}") for k in range(CB)]
-        w_out_sb = held.tile([P, FB, C], BF16, name="w_out_sb")
+        pos = held.tile([P, CB, N], F32, name="pos")
+        w_in_sb = held.tile([P, CB, 2 * F], BF16, name="w_in_sb")
+        w_out_sb = held.tile([P, FB, P, CB], BF16, name="w_out_sb")
         x32 = [held.tile([P, N], F32, name=f"x32_{k}") for k in range(CB)]
         x16 = [held.tile([P, N], BF16, name=f"x16_{k}") for k in range(CB)]
         h = [held.tile([P, N], BF16, name=f"h{f}") for f in range(FB)]
 
         nc.sync.dma_start(offsets[:], offs)
-        for k in range(CB - 1):
-            nc.sync.dma_start(pos[k][:], pos_enc[k * P : (k + 1) * P, :])
-            nc.sync.dma_start(table[k][:], tok_emb[k * P : (k + 1) * P, :])
-        for k in range(CB - 1):
-            nc.sync.dma_start(w_in_sb[k][:], w_in[k * P : (k + 1) * P, :])
-        nc.sync.dma_start(pos[CB - 1][:], pos_enc[(CB - 1) * P :, :])
-        nc.sync.dma_start(table[CB - 1][:], tok_emb[(CB - 1) * P :, :])
-        nc.sync.dma_start(w_in_sb[CB - 1][:], w_in[(CB - 1) * P :, :])
-        nc.sync.dma_start(w_out_sb[:], w_out.rearrange("(f p) c -> p f c", p=P))
+        nc.sync.dma_start(pos[:], pos_rows)
+        for k in range(CB - 2):
+            nc.sync.dma_start(table[k][:], tok_blocks[k])
+        nc.sync.dma_start(table[CB - 2][:, : S // 2], tok_blocks[CB - 2][:, : S // 2])
+        nc.sync.dma_start(w_in_sb[:, : CB - 1, :], w_in_rows[:, : CB - 1, :])
+        nc.sync.dma_start(table[CB - 2][:, S // 2 :], tok_blocks[CB - 2][:, S // 2 :])
+        nc.sync.dma_start(table[CB - 1][:], tok_blocks[CB - 1])
+        nc.sync.dma_start(w_in_sb[:, CB - 1, :], w_in_rows[:, CB - 1, :])
+        nc.sync.dma_start(w_out_sb[:], w_out_rows)
 
         gate = []
         val = []
@@ -58,16 +63,16 @@ def tile_vanillatransformer_kernel(tc, tok_emb, pos_enc, w_in, w_out, offs, out)
                 nc.vector.tensor_tensor(
                     x32[k][:, cols],
                     table[k][:].indirect(offsets[:, t * width // 16 : (t + 1) * width // 16]),
-                    pos[k][:, cols],
+                    pos[:, k, cols],
                     ADD,
                 )
                 nc.scalar.activation(x16[k][:, cols], x32[k][:, cols], COPY)
             for f in range(FB):
                 nc.tensor.matmul(
-                    gate[f][:], w_in_sb[k][:, f * P : (f + 1) * P], x16[k][:], start=k == 0, stop=k == CB - 1
+                    gate[f][:], w_in_sb[:, k, f * P : (f + 1) * P], x16[k][:], start=k == 0, stop=k == CB - 1
                 )
                 nc.tensor.matmul(
-                    val[f][:], w_in_sb[k][:, F + f * P : F + (f + 1) * P], x16[k][:], start=k == 0, stop=k == CB - 1
+                    val[f][:], w_in_sb[:, k, F + f * P : F + (f + 1) * P], x16[k][:], start=k == 0, stop=k == CB - 1
                 )
 
         for f in range(FB):
@@ -78,12 +83,10 @@ def tile_vanillatransformer_kernel(tc, tok_emb, pos_enc, w_in, w_out, offs, out)
         ffn = [psum.tile([P, N], F32, name=f"ffn{m}", tag="bank") for m in range(CB)]
         for f in range(FB // 2):
             for m in range(CB):
-                nc.tensor.matmul(ffn[m][:], w_out_sb[:, f, m * P : (m + 1) * P], h[f][:], start=f == 0, stop=False)
+                nc.tensor.matmul(ffn[m][:], w_out_sb[:, f, :, m], h[f][:], start=f == 0, stop=False)
         for m in range(CB):
             for f in range(FB // 2, FB):
-                nc.tensor.matmul(
-                    ffn[m][:], w_out_sb[:, f, m * P : (m + 1) * P], h[f][:], start=False, stop=f == FB - 1
-                )
+                nc.tensor.matmul(ffn[m][:], w_out_sb[:, f, :, m], h[f][:], start=False, stop=f == FB - 1)
             result = work.tile([P, N], F32, name="result")
             nc.vector.tensor_tensor(result[:], ffn[m][:], x32[m][:], ADD)
-            nc.sync.dma_start(out[m * P : (m + 1) * P, :], result[:])
+            nc.sync.dma_start(out_blocks[m], result[:])

@@ -40,7 +40,8 @@ def tile_vanillatransformer_kernel(tc, tok_emb, pos_enc, w_in, w_out, offs, out)
         h = [held.tile([P, N], BF16, name=f"h{f}") for f in range(FB)]
 
         nc.sync.dma_start(offsets[:], offs)
-        nc.sync.dma_start(pos[:], pos_rows)
+        nc.gpsimd.memset(pos[:], 0.0)
+        nc.sync.dma_start(pos[0:1, :, :], pos_rows[0:1, :, :])
         for k in range(CB - 2):
             nc.sync.dma_start(table[k][:], tok_blocks[k])
         nc.sync.dma_start(table[CB - 2][:, : S // 2], tok_blocks[CB - 2][:, : S // 2])

@@ -27,7 +27,7 @@ def tile_vanillatransformer_kernel(tc, tok_emb, pos_enc, w_in, w_out, offs, out)
     w_out_rows = w_out.rearrange("(f p) (q k) -> p f q k", p=P, k=CB)
     with (
         tc.tile_pool(name="held", bufs=1) as held,
-        tc.tile_pool(name="work", bufs=4) as work,
+        tc.tile_pool(name="work", bufs=CB + 1) as work,
         tc.psum_pool(name="psum", bufs=BANKS) as psum,
     ):
         offsets = held.tile([P, N // 16], U16, name="offsets")
@@ -39,10 +39,11 @@ def tile_vanillatransformer_kernel(tc, tok_emb, pos_enc, w_in, w_out, offs, out)
         x16 = [held.tile([P, N], BF16, name=f"x16_{k}") for k in range(CB)]
         h = [held.tile([P, N], BF16, name=f"h{f}") for f in range(FB)]
 
+        nc.sync.dma_start(table[0][:], tok_blocks[0])
         nc.sync.dma_start(offsets[:], offs)
         nc.gpsimd.memset(pos[:], 0.0)
         nc.sync.dma_start(pos[0:1, :, :], pos_rows[0:1, :, :])
-        for k in range(CB - 2):
+        for k in range(1, CB - 2):
             nc.sync.dma_start(table[k][:], tok_blocks[k])
         nc.sync.dma_start(table[CB - 2][:, : S // 2], tok_blocks[CB - 2][:, : S // 2])
         nc.sync.dma_start(w_in_sb[:, : CB - 1, :], w_in_rows[:, : CB - 1, :])
@@ -81,13 +82,13 @@ def tile_vanillatransformer_kernel(tc, tok_emb, pos_enc, w_in, w_out, offs, out)
             nc.scalar.activation(relu_gate[:], gate[f][:], RELU)
             nc.vector.tensor_tensor(h[f][:], relu_gate[:], val[f][:], MULT)
 
-        ffn = [psum.tile([P, N], F32, name=f"ffn{m}", tag="bank") for m in range(CB)]
-        for f in range(FB // 2):
-            for m in range(CB):
-                nc.tensor.matmul(ffn[m][:], w_out_sb[:, f, :, m], h[f][:], start=f == 0, stop=False)
-        for m in range(CB):
-            for f in range(FB // 2, FB):
-                nc.tensor.matmul(ffn[m][:], w_out_sb[:, f, :, m], h[f][:], start=False, stop=f == FB - 1)
+        units = [(m, slice(0, N)) for m in range(CB - 1)] + [(CB - 1, slice(0, N // 2)), (CB - 1, slice(N // 2, N))]
+        ffn = [psum.tile([P, N], F32, name=f"ffn{u}", tag="bank") for u in range(len(units))]
+        for u, (m, cols) in enumerate(units):
+            nc.tensor.matmul(ffn[u][:, cols], w_out_sb[:, 0, :, m], h[0][:, cols], start=True, stop=False)
+        for u, (m, cols) in enumerate(units):
+            for f in range(1, FB):
+                nc.tensor.matmul(ffn[u][:, cols], w_out_sb[:, f, :, m], h[f][:, cols], start=False, stop=f == FB - 1)
             result = work.tile([P, N], F32, name="result")
-            nc.vector.tensor_tensor(result[:], ffn[m][:], x32[m][:], ADD)
-            nc.sync.dma_start(out_blocks[m], result[:])
+            nc.vector.tensor_tensor(result[:, cols], ffn[u][:, cols], x32[m][:, cols], ADD)
+            nc.sync.dma_start(out_blocks[m][:, cols], result[:, cols])

@@ -14,6 +14,7 @@ CB = C // P
 FB = F // P
 BANKS = 8
 LAST_CUTS = 4
+EARLY = (CB - 2) * 2 * F + F
 
 FLOPS = 2 * C * (2 * F) * N + 2 * F * C * N
 
@@ -23,7 +24,7 @@ def tile_vanillatransformer_kernel(tc, tok_emb, pos_enc, w_in, w_out, offs, out)
     tok_blocks = tok_emb.rearrange("(p k) s -> k p s", k=CB)
     out_blocks = out.rearrange("(p k) j -> k p j", k=CB)
     pos_rows = pos_enc.rearrange("(p k) j -> p k j", k=CB)
-    w_in_rows = w_in.rearrange("(p k) f -> p k f", k=CB)
+    w_in_rows = w_in.rearrange("(p k) f -> p (k f)", k=CB)
     w_out_rows = w_out.rearrange("(f p) (q k) -> p f q k", p=P, k=CB)
     with (
         tc.tile_pool(name="held", bufs=1) as held,
@@ -33,7 +34,7 @@ def tile_vanillatransformer_kernel(tc, tok_emb, pos_enc, w_in, w_out, offs, out)
         offsets = held.tile([P, N // 16], U16, name="offsets")
         table = [held.tile([P, S], F32, name=f"table{k}") for k in range(CB)]
         pos = held.tile([P, CB, N], F32, name="pos")
-        w_in_sb = held.tile([P, CB, 2 * F], BF16, name="w_in_sb")
+        w_in_sb = held.tile([P, CB * 2 * F], BF16, name="w_in_sb")
         w_out_sb = held.tile([P, FB, P, CB], BF16, name="w_out_sb")
         x32 = [held.tile([P, N], F32, name=f"x32_{k}") for k in range(CB)]
         x16 = [held.tile([P, N], BF16, name=f"x16_{k}") for k in range(CB)]
@@ -46,10 +47,11 @@ def tile_vanillatransformer_kernel(tc, tok_emb, pos_enc, w_in, w_out, offs, out)
         for k in range(1, CB - 2):
             nc.sync.dma_start(table[k][:], tok_blocks[k])
         nc.sync.dma_start(table[CB - 2][:, : S // 2], tok_blocks[CB - 2][:, : S // 2])
-        nc.sync.dma_start(w_in_sb[:, : CB - 1, :], w_in_rows[:, : CB - 1, :])
+        nc.sync.dma_start(w_in_sb[:, :EARLY], w_in_rows[:, :EARLY])
         nc.sync.dma_start(table[CB - 2][:, S // 2 :], tok_blocks[CB - 2][:, S // 2 :])
         nc.sync.dma_start(table[CB - 1][:], tok_blocks[CB - 1])
-        nc.sync.dma_start(w_in_sb[:, CB - 1, :], w_in_rows[:, CB - 1, :])
+        nc.sync.dma_start(w_in_sb[:, EARLY : (CB - 1) * 2 * F], w_in_rows[:, EARLY : (CB - 1) * 2 * F])
+        nc.sync.dma_start(w_in_sb[:, (CB - 1) * 2 * F :], w_in_rows[:, (CB - 1) * 2 * F :])
         nc.sync.dma_start(w_out_sb[:], w_out_rows)
 
         gate = []
@@ -69,13 +71,13 @@ def tile_vanillatransformer_kernel(tc, tok_emb, pos_enc, w_in, w_out, offs, out)
                     ADD,
                 )
                 nc.scalar.activation(x16[k][:, cols], x32[k][:, cols], COPY)
-            for f in range(FB):
-                nc.tensor.matmul(
-                    gate[f][:], w_in_sb[:, k, f * P : (f + 1) * P], x16[k][:], start=k == 0, stop=k == CB - 1
-                )
-                nc.tensor.matmul(
-                    val[f][:], w_in_sb[:, k, F + f * P : F + (f + 1) * P], x16[k][:], start=k == 0, stop=k == CB - 1
-                )
+            products = [(gate[f], k * 2 * F + f * P) for f in range(FB)] + [
+                (val[f], k * 2 * F + F + f * P) for f in range(FB)
+            ]
+            if k != CB - 2:
+                products = [products[i // 2 + (i % 2) * FB] for i in range(2 * FB)]
+            for bank, col in products:
+                nc.tensor.matmul(bank[:], w_in_sb[:, col : col + P], x16[k][:], start=k == 0, stop=k == CB - 1)
 
         for f in range(FB):
             relu_gate = work.tile([P, N], F32, name="relu_gate")

@@ -13,8 +13,10 @@ C, S, N, F = 512, 4096, 512, 512
 CB = C // P
 FB = F // P
 BANKS = 8
+HALVES = 2
+NH = N // HALVES
 LAST_CUTS = 4
-EARLY = (CB - 2) * 2 * F + F
+EARLY = (CB - 1) * 2 * F
 
 FLOPS = 2 * C * (2 * F) * N + 2 * F * C * N
 
@@ -28,7 +30,7 @@ def tile_vanillatransformer_kernel(tc, tok_emb, pos_enc, w_in, w_out, offs, out)
     w_out_rows = w_out.rearrange("(f p) (q k) -> p f q k", p=P, k=CB)
     with (
         tc.tile_pool(name="held", bufs=1) as held,
-        tc.tile_pool(name="work", bufs=CB + 1) as work,
+        tc.tile_pool(name="work", bufs=HALVES * CB) as work,
         tc.psum_pool(name="psum", bufs=BANKS) as psum,
     ):
         offsets = held.tile([P, N // 16], U16, name="offsets")
@@ -38,7 +40,7 @@ def tile_vanillatransformer_kernel(tc, tok_emb, pos_enc, w_in, w_out, offs, out)
         w_out_sb = held.tile([P, FB, P, CB], BF16, name="w_out_sb")
         x32 = [held.tile([P, N], F32, name=f"x32_{k}") for k in range(CB)]
         x16 = [held.tile([P, N], BF16, name=f"x16_{k}") for k in range(CB)]
-        h = [held.tile([P, N], BF16, name=f"h{f}") for f in range(FB)]
+        h = [[held.tile([P, NH], BF16, name=f"h{a}_{f}") for f in range(FB)] for a in range(HALVES)]
 
         nc.sync.dma_start(table[0][:], tok_blocks[0])
         nc.sync.dma_start(offsets[:], offs)
@@ -46,19 +48,16 @@ def tile_vanillatransformer_kernel(tc, tok_emb, pos_enc, w_in, w_out, offs, out)
         nc.sync.dma_start(pos[0:1, :, :], pos_rows[0:1, :, :])
         for k in range(1, CB - 2):
             nc.sync.dma_start(table[k][:], tok_blocks[k])
-        nc.sync.dma_start(table[CB - 2][:, : S // 2], tok_blocks[CB - 2][:, : S // 2])
         nc.sync.dma_start(w_in_sb[:, :EARLY], w_in_rows[:, :EARLY])
-        nc.sync.dma_start(table[CB - 2][:, S // 2 :], tok_blocks[CB - 2][:, S // 2 :])
+        nc.sync.dma_start(table[CB - 2][:], tok_blocks[CB - 2])
         nc.sync.dma_start(table[CB - 1][:], tok_blocks[CB - 1])
-        nc.sync.dma_start(w_in_sb[:, EARLY : (CB - 1) * 2 * F], w_in_rows[:, EARLY : (CB - 1) * 2 * F])
-        nc.sync.dma_start(w_in_sb[:, (CB - 1) * 2 * F :], w_in_rows[:, (CB - 1) * 2 * F :])
+        nc.sync.dma_start(w_in_sb[:, EARLY:], w_in_rows[:, EARLY:])
         nc.sync.dma_start(w_out_sb[:], w_out_rows)
 
-        gate = []
-        val = []
-        for f in range(FB):
-            gate.append(psum.tile([P, N], F32, name=f"gate{f}", tag="bank"))
-            val.append(psum.tile([P, N], F32, name=f"val{f}", tag="bank"))
+        gate_val = [
+            [psum.tile([P, 2 * NH], F32, name=f"gate_val{a}_{f}", tag="bank") for f in range(FB)]
+            for a in range(HALVES)
+        ]
         for k in range(CB):
             cuts = LAST_CUTS if k == CB - 1 else 1
             width = N // cuts
@@ -71,26 +70,38 @@ def tile_vanillatransformer_kernel(tc, tok_emb, pos_enc, w_in, w_out, offs, out)
                     ADD,
                 )
                 nc.scalar.activation(x16[k][:, cols], x32[k][:, cols], COPY)
-            products = [(gate[f], k * 2 * F + f * P) for f in range(FB)] + [
-                (val[f], k * 2 * F + F + f * P) for f in range(FB)
-            ]
-            if k != CB - 2:
-                products = [products[i // 2 + (i % 2) * FB] for i in range(2 * FB)]
-            for bank, col in products:
-                nc.tensor.matmul(bank[:], w_in_sb[:, col : col + P], x16[k][:], start=k == 0, stop=k == CB - 1)
+            for a in range(HALVES):
+                tokens = slice(a * NH, (a + 1) * NH)
+                for f in range(FB):
+                    gate_col = k * 2 * F + f * P
+                    val_col = gate_col + F
+                    nc.tensor.matmul(
+                        gate_val[a][f][:, :NH],
+                        w_in_sb[:, gate_col : gate_col + P],
+                        x16[k][:, tokens],
+                        start=k == 0,
+                        stop=False,
+                    )
+                    nc.tensor.matmul(
+                        gate_val[a][f][:, NH:],
+                        w_in_sb[:, val_col : val_col + P],
+                        x16[k][:, tokens],
+                        start=False,
+                        stop=k == CB - 1,
+                    )
 
-        for f in range(FB):
-            relu_gate = work.tile([P, N], F32, name="relu_gate")
-            nc.scalar.activation(relu_gate[:], gate[f][:], RELU)
-            nc.vector.tensor_tensor(h[f][:], relu_gate[:], val[f][:], MULT)
+        for a in range(HALVES):
+            for f in range(FB):
+                relu_gate = work.tile([P, NH], F32, name="relu_gate")
+                nc.scalar.activation(relu_gate[:], gate_val[a][f][:, :NH], RELU)
+                nc.vector.tensor_tensor(h[a][f][:], relu_gate[:], gate_val[a][f][:, NH:], MULT)
 
-        units = [(m, slice(0, N)) for m in range(CB - 1)] + [(CB - 1, slice(0, N // 2)), (CB - 1, slice(N // 2, N))]
-        ffn = [psum.tile([P, N], F32, name=f"ffn{u}", tag="bank") for u in range(len(units))]
-        for u, (m, cols) in enumerate(units):
-            nc.tensor.matmul(ffn[u][:, cols], w_out_sb[:, 0, :, m], h[0][:, cols], start=True, stop=False)
-        for u, (m, cols) in enumerate(units):
-            for f in range(1, FB):
-                nc.tensor.matmul(ffn[u][:, cols], w_out_sb[:, f, :, m], h[f][:, cols], start=False, stop=f == FB - 1)
-            result = work.tile([P, N], F32, name="result")
-            nc.vector.tensor_tensor(result[:, cols], ffn[u][:, cols], x32[m][:, cols], ADD)
-            nc.sync.dma_start(out_blocks[m][:, cols], result[:, cols])
+        for a in range(HALVES):
+            tokens = slice(a * NH, (a + 1) * NH)
+            for m in range(CB):
+                ffn = psum.tile([P, NH], F32, name="ffn", tag="bank")
+                for f in range(FB):
+                    nc.tensor.matmul(ffn[:], w_out_sb[:, f, :, m], h[a][f][:], start=f == 0, stop=f == FB - 1)
+                result = work.tile([P, NH], F32, name="result")
+                nc.vector.tensor_tensor(result[:], ffn[:], x32[m][:, tokens], ADD)
+                nc.sync.dma_start(out_blocks[m][:, tokens], result[:])

@@ -16,7 +16,9 @@ BANKS = 8
 HALVES = 2
 NH = N // HALVES
 LAST_CUTS = 4
-EARLY = (CB - 1) * 2 * F
+BLOCK3 = (CB - 1) * 2 * F
+LATE_VAL = 2
+EARLY = BLOCK3 - LATE_VAL * P
 
 FLOPS = 2 * C * (2 * F) * N + 2 * F * C * N
 
@@ -51,7 +53,8 @@ def tile_vanillatransformer_kernel(tc, tok_emb, pos_enc, w_in, w_out, offs, out)
         nc.sync.dma_start(w_in_sb[:, :EARLY], w_in_rows[:, :EARLY])
         nc.sync.dma_start(table[CB - 2][:], tok_blocks[CB - 2])
         nc.sync.dma_start(table[CB - 1][:], tok_blocks[CB - 1])
-        nc.sync.dma_start(w_in_sb[:, EARLY:], w_in_rows[:, EARLY:])
+        nc.sync.dma_start(w_in_sb[:, EARLY:BLOCK3], w_in_rows[:, EARLY:BLOCK3])
+        nc.sync.dma_start(w_in_sb[:, BLOCK3:], w_in_rows[:, BLOCK3:])
         nc.sync.dma_start(w_out_sb[:], w_out_rows)
 
         gate_val = [
@@ -70,25 +73,18 @@ def tile_vanillatransformer_kernel(tc, tok_emb, pos_enc, w_in, w_out, offs, out)
                     ADD,
                 )
                 nc.scalar.activation(x16[k][:, cols], x32[k][:, cols], COPY)
-            for a in range(HALVES):
-                tokens = slice(a * NH, (a + 1) * NH)
-                for f in range(FB):
-                    gate_col = k * 2 * F + f * P
-                    val_col = gate_col + F
-                    nc.tensor.matmul(
-                        gate_val[a][f][:, :NH],
-                        w_in_sb[:, gate_col : gate_col + P],
-                        x16[k][:, tokens],
-                        start=k == 0,
-                        stop=False,
-                    )
-                    nc.tensor.matmul(
-                        gate_val[a][f][:, NH:],
-                        w_in_sb[:, val_col : val_col + P],
-                        x16[k][:, tokens],
-                        start=False,
-                        stop=k == CB - 1,
-                    )
+            products = [(a, f, v) for a in range(HALVES) for f in range(FB) for v in range(2)]
+            if k == CB - 2:
+                products = sorted(products, key=lambda afv: afv[2] == 1 and afv[1] >= FB - LATE_VAL)
+            for a, f, v in products:
+                col = k * 2 * F + v * F + f * P
+                nc.tensor.matmul(
+                    gate_val[a][f][:, v * NH : (v + 1) * NH],
+                    w_in_sb[:, col : col + P],
+                    x16[k][:, a * NH : (a + 1) * NH],
+                    start=k == 0 and v == 0,
+                    stop=k == CB - 1 and v == 1,
+                )
 
         for a in range(HALVES):
             for f in range(FB):

@@ -16,20 +16,19 @@ BANKS = 8
 HALVES = 2
 NH = N // HALVES
 LAST_CUTS = 4
-BLOCK3 = (CB - 1) * 2 * F
+POS_ROWS = 4
 LATE_VAL = 2
-EARLY = BLOCK3 - LATE_VAL * P
+EARLY = 2 * F - LATE_VAL * P
 
 FLOPS = 2 * C * (2 * F) * N + 2 * F * C * N
 
 
 def tile_vanillatransformer_kernel(tc, tok_emb, pos_enc, w_in, w_out, offs, out):
     nc = tc.nc
-    tok_blocks = tok_emb.rearrange("(p k) s -> k p s", k=CB)
-    out_blocks = out.rearrange("(p k) j -> k p j", k=CB)
-    pos_rows = pos_enc.rearrange("(p k) j -> p k j", k=CB)
-    w_in_rows = w_in.rearrange("(p k) f -> p (k f)", k=CB)
-    w_out_rows = w_out.rearrange("(f p) (q k) -> p f q k", p=P, k=CB)
+    tok_blocks = tok_emb.rearrange("(k p) s -> k p s", p=P)
+    out_blocks = out.rearrange("(k p) j -> k p j", p=P)
+    w_in_rows = w_in.rearrange("(k p) f -> p k f", p=P)
+    w_out_rows = w_out.rearrange("(f p) c -> p f c", p=P)
     with (
         tc.tile_pool(name="held", bufs=1) as held,
         tc.tile_pool(name="work", bufs=HALVES * CB) as work,
@@ -37,24 +36,27 @@ def tile_vanillatransformer_kernel(tc, tok_emb, pos_enc, w_in, w_out, offs, out)
     ):
         offsets = held.tile([P, N // 16], U16, name="offsets")
         table = [held.tile([P, S], F32, name=f"table{k}") for k in range(CB)]
-        pos = held.tile([P, CB, N], F32, name="pos")
-        w_in_sb = held.tile([P, CB * 2 * F], BF16, name="w_in_sb")
-        w_out_sb = held.tile([P, FB, P, CB], BF16, name="w_out_sb")
+        pos0 = held.tile([P, N], F32, name="pos0")
+        zeros = held.tile([P, N], F32, name="zeros")
+        w_in_sb = held.tile([P, CB, 2 * F], BF16, name="w_in_sb")
+        w_out_sb = held.tile([P, FB, C], BF16, name="w_out_sb")
         x32 = [held.tile([P, N], F32, name=f"x32_{k}") for k in range(CB)]
         x16 = [held.tile([P, N], BF16, name=f"x16_{k}") for k in range(CB)]
         h = [[held.tile([P, NH], BF16, name=f"h{a}_{f}") for f in range(FB)] for a in range(HALVES)]
 
         nc.sync.dma_start(table[0][:], tok_blocks[0])
         nc.sync.dma_start(offsets[:], offs)
-        nc.gpsimd.memset(pos[:], 0.0)
-        nc.sync.dma_start(pos[0:1, :, :], pos_rows[0:1, :, :])
+        nc.gpsimd.memset(pos0[:], 0.0)
+        nc.gpsimd.memset(zeros[:], 0.0)
+        nc.sync.dma_start(pos0[:POS_ROWS, :], pos_enc[:POS_ROWS, :])
         for k in range(1, CB - 2):
             nc.sync.dma_start(table[k][:], tok_blocks[k])
-        nc.sync.dma_start(w_in_sb[:, :EARLY], w_in_rows[:, :EARLY])
+        nc.sync.dma_start(w_in_sb[:, : CB - 2, :], w_in_rows[:, : CB - 2, :])
+        nc.sync.dma_start(w_in_sb[:, CB - 2, :EARLY], w_in_rows[:, CB - 2, :EARLY])
         nc.sync.dma_start(table[CB - 2][:], tok_blocks[CB - 2])
         nc.sync.dma_start(table[CB - 1][:], tok_blocks[CB - 1])
-        nc.sync.dma_start(w_in_sb[:, EARLY:BLOCK3], w_in_rows[:, EARLY:BLOCK3])
-        nc.sync.dma_start(w_in_sb[:, BLOCK3:], w_in_rows[:, BLOCK3:])
+        nc.sync.dma_start(w_in_sb[:, CB - 2, EARLY:], w_in_rows[:, CB - 2, EARLY:])
+        nc.sync.dma_start(w_in_sb[:, CB - 1, :], w_in_rows[:, CB - 1, :])
         nc.sync.dma_start(w_out_sb[:], w_out_rows)
 
         gate_val = [
@@ -69,7 +71,7 @@ def tile_vanillatransformer_kernel(tc, tok_emb, pos_enc, w_in, w_out, offs, out)
                 nc.vector.tensor_tensor(
                     x32[k][:, cols],
                     table[k][:].indirect(offsets[:, t * width // 16 : (t + 1) * width // 16]),
-                    pos[:, k, cols],
+                    pos0[:, cols] if k == 0 else zeros[:, cols],
                     ADD,
                 )
                 nc.scalar.activation(x16[k][:, cols], x32[k][:, cols], COPY)
@@ -77,10 +79,10 @@ def tile_vanillatransformer_kernel(tc, tok_emb, pos_enc, w_in, w_out, offs, out)
             if k == CB - 2:
                 products = sorted(products, key=lambda afv: afv[2] == 1 and afv[1] >= FB - LATE_VAL)
             for a, f, v in products:
-                col = k * 2 * F + v * F + f * P
+                col = v * F + f * P
                 nc.tensor.matmul(
                     gate_val[a][f][:, v * NH : (v + 1) * NH],
-                    w_in_sb[:, col : col + P],
+                    w_in_sb[:, k, col : col + P],
                     x16[k][:, a * NH : (a + 1) * NH],
                     start=k == 0 and v == 0,
                     stop=k == CB - 1 and v == 1,
@@ -97,7 +99,7 @@ def tile_vanillatransformer_kernel(tc, tok_emb, pos_enc, w_in, w_out, offs, out)
             for m in range(CB):
                 ffn = psum.tile([P, NH], F32, name="ffn", tag="bank")
                 for f in range(FB):
-                    nc.tensor.matmul(ffn[:], w_out_sb[:, f, :, m], h[a][f][:], start=f == 0, stop=f == FB - 1)
+                    nc.tensor.matmul(ffn[:], w_out_sb[:, f, m * P : (m + 1) * P], h[a][f][:], start=f == 0, stop=f == FB - 1)
                 result = work.tile([P, NH], F32, name="result")
                 nc.vector.tensor_tensor(result[:], ffn[:], x32[m][:, tokens], ADD)
                 nc.sync.dma_start(out_blocks[m][:, tokens], result[:])

@@ -94,12 +94,19 @@ def tile_vanillatransformer_kernel(tc, tok_emb, pos_enc, w_in, w_out, offs, out)
                 nc.scalar.activation(relu_gate[:], gate_val[a][f][:, :NH], RELU)
                 nc.vector.tensor_tensor(h[a][f][:], relu_gate[:], gate_val[a][f][:, NH:], MULT)
 
-        for a in range(HALVES):
-            tokens = slice(a * NH, (a + 1) * NH)
-            for m in range(CB):
-                ffn = psum.tile([P, NH], F32, name="ffn", tag="bank")
-                for f in range(FB):
-                    nc.tensor.matmul(ffn[:], w_out_sb[:, f, m * P : (m + 1) * P], h[a][f][:], start=f == 0, stop=f == FB - 1)
-                result = work.tile([P, NH], F32, name="result")
-                nc.vector.tensor_tensor(result[:], ffn[:], x32[m][:, tokens], ADD)
-                nc.sync.dma_start(out_blocks[m][:, tokens], result[:])
+        units = [(a, m, 0, NH) for a in range(HALVES) for m in range(CB)]
+        units = units[:-1] + [(HALVES - 1, CB - 1, 0, NH // 2), (HALVES - 1, CB - 1, NH // 2, NH)]
+        for a, m, lo, hi in units:
+            tokens = slice(a * NH + lo, a * NH + hi)
+            ffn = psum.tile([P, NH], F32, name="ffn", tag="bank")
+            for f in range(FB):
+                nc.tensor.matmul(
+                    ffn[:, : hi - lo],
+                    w_out_sb[:, f, m * P : (m + 1) * P],
+                    h[a][f][:, lo:hi],
+                    start=f == 0,
+                    stop=f == FB - 1,
+                )
+            result = work.tile([P, NH], F32, name="result")
+            nc.vector.tensor_tensor(result[:, : hi - lo], ffn[:, : hi - lo], x32[m][:, tokens], ADD)
+            nc.sync.dma_start(out_blocks[m][:, tokens], result[:, : hi - lo])

@@ -17,7 +17,7 @@ HALVES = 2
 NH = N // HALVES
 LAST_CUTS = 4
 POS_ROWS = 4
-LATE_VAL = 2
+LATE_VAL = 4
 EARLY = 2 * F - LATE_VAL * P
 
 FLOPS = 2 * C * (2 * F) * N + 2 * F * C * N

@@ -16,19 +16,20 @@ BANKS = 8
 HALVES = 2
 NH = N // HALVES
 LAST_CUTS = 4
-POS_ROWS = 4
+BLOCK3 = (CB - 1) * 2 * F
 LATE_VAL = 4
-EARLY = 2 * F - LATE_VAL * P
+EARLY = BLOCK3 - LATE_VAL * P
 
 FLOPS = 2 * C * (2 * F) * N + 2 * F * C * N
 
 
 def tile_vanillatransformer_kernel(tc, tok_emb, pos_enc, w_in, w_out, offs, out):
     nc = tc.nc
-    tok_blocks = tok_emb.rearrange("(k p) s -> k p s", p=P)
-    out_blocks = out.rearrange("(k p) j -> k p j", p=P)
-    w_in_rows = w_in.rearrange("(k p) f -> p k f", p=P)
-    w_out_rows = w_out.rearrange("(f p) c -> p f c", p=P)
+    tok_blocks = tok_emb.rearrange("(p k) s -> k p s", k=CB)
+    out_blocks = out.rearrange("(p k) j -> k p j", k=CB)
+    pos_rows = pos_enc.rearrange("(p k) j -> p k j", k=CB)
+    w_in_rows = w_in.rearrange("(p k) f -> p (k f)", k=CB)
+    w_out_rows = w_out.rearrange("(f p) (q k) -> p f q k", p=P, k=CB)
     with (
         tc.tile_pool(name="held", bufs=1) as held,
         tc.tile_pool(name="work", bufs=HALVES * CB) as work,
@@ -36,27 +37,24 @@ def tile_vanillatransformer_kernel(tc, tok_emb, pos_enc, w_in, w_out, offs, out)
     ):
         offsets = held.tile([P, N // 16], U16, name="offsets")
         table = [held.tile([P, S], F32, name=f"table{k}") for k in range(CB)]
-        pos0 = held.tile([P, N], F32, name="pos0")
-        zeros = held.tile([P, N], F32, name="zeros")
-        w_in_sb = held.tile([P, CB, 2 * F], BF16, name="w_in_sb")
-        w_out_sb = held.tile([P, FB, C], BF16, name="w_out_sb")
+        pos = held.tile([P, CB, N], F32, name="pos")
+        w_in_sb = held.tile([P, CB * 2 * F], BF16, name="w_in_sb")
+        w_out_sb = held.tile([P, FB, P, CB], BF16, name="w_out_sb")
         x32 = [held.tile([P, N], F32, name=f"x32_{k}") for k in range(CB)]
         x16 = [held.tile([P, N], BF16, name=f"x16_{k}") for k in range(CB)]
         h = [[held.tile([P, NH], BF16, name=f"h{a}_{f}") for f in range(FB)] for a in range(HALVES)]
 
         nc.sync.dma_start(table[0][:], tok_blocks[0])
         nc.sync.dma_start(offsets[:], offs)
-        nc.gpsimd.memset(pos0[:], 0.0)
-        nc.gpsimd.memset(zeros[:], 0.0)
-        nc.sync.dma_start(pos0[:POS_ROWS, :], pos_enc[:POS_ROWS, :])
+        nc.gpsimd.memset(pos[:], 0.0)
+        nc.sync.dma_start(pos[0:1, :, :], pos_rows[0:1, :, :])
         for k in range(1, CB - 2):
             nc.sync.dma_start(table[k][:], tok_blocks[k])
-        nc.sync.dma_start(w_in_sb[:, : CB - 2, :], w_in_rows[:, : CB - 2, :])
-        nc.sync.dma_start(w_in_sb[:, CB - 2, :EARLY], w_in_rows[:, CB - 2, :EARLY])
+        nc.sync.dma_start(w_in_sb[:, :EARLY], w_in_rows[:, :EARLY])
         nc.sync.dma_start(table[CB - 2][:], tok_blocks[CB - 2])
         nc.sync.dma_start(table[CB - 1][:], tok_blocks[CB - 1])
-        nc.sync.dma_start(w_in_sb[:, CB - 2, EARLY:], w_in_rows[:, CB - 2, EARLY:])
-        nc.sync.dma_start(w_in_sb[:, CB - 1, :], w_in_rows[:, CB - 1, :])
+        nc.sync.dma_start(w_in_sb[:, EARLY:BLOCK3], w_in_rows[:, EARLY:BLOCK3])
+        nc.sync.dma_start(w_in_sb[:, BLOCK3:], w_in_rows[:, BLOCK3:])
         nc.sync.dma_start(w_out_sb[:], w_out_rows)
 
         gate_val = [
@@ -71,7 +69,7 @@ def tile_vanillatransformer_kernel(tc, tok_emb, pos_enc, w_in, w_out, offs, out)
                 nc.vector.tensor_tensor(
                     x32[k][:, cols],
                     table[k][:].indirect(offsets[:, t * width // 16 : (t + 1) * width // 16]),
-                    pos0[:, cols] if k == 0 else zeros[:, cols],
+                    pos[:, k, cols],
                     ADD,
                 )
                 nc.scalar.activation(x16[k][:, cols], x32[k][:, cols], COPY)
@@ -79,10 +77,10 @@ def tile_vanillatransformer_kernel(tc, tok_emb, pos_enc, w_in, w_out, offs, out)
             if k == CB - 2:
                 products = sorted(products, key=lambda afv: afv[2] == 1 and afv[1] >= FB - LATE_VAL)
             for a, f, v in products:
-                col = v * F + f * P
+                col = k * 2 * F + v * F + f * P
                 nc.tensor.matmul(
                     gate_val[a][f][:, v * NH : (v + 1) * NH],
-                    w_in_sb[:, k, col : col + P],
+                    w_in_sb[:, col : col + P],
                     x16[k][:, a * NH : (a + 1) * NH],
                     start=k == 0 and v == 0,
                     stop=k == CB - 1 and v == 1,
@@ -101,11 +99,7 @@ def tile_vanillatransformer_kernel(tc, tok_emb, pos_enc, w_in, w_out, offs, out)
             ffn = psum.tile([P, NH], F32, name="ffn", tag="bank")
             for f in range(FB):
                 nc.tensor.matmul(
-                    ffn[:, : hi - lo],
-                    w_out_sb[:, f, m * P : (m + 1) * P],
-                    h[a][f][:, lo:hi],
-                    start=f == 0,
-                    stop=f == FB - 1,
+                    ffn[:, : hi - lo], w_out_sb[:, f, :, m], h[a][f][:, lo:hi], start=f == 0, stop=f == FB - 1
                 )
             result = work.tile([P, NH], F32, name="result")
             nc.vector.tensor_tensor(result[:, : hi - lo], ffn[:, : hi - lo], x32[m][:, tokens], ADD)

import concourse.mybir as mybir

F32 = mybir.dt.float32
BF16 = mybir.dt.bfloat16
U16 = mybir.dt.uint16
ADD = mybir.AluOpType.add
MULT = mybir.AluOpType.mult
COPY = mybir.ActivationFunctionType.Copy
RELU = mybir.ActivationFunctionType.Relu

P = 128
C, S, N, F = 512, 4096, 512, 512
CB = C // P
FB = F // P
BANKS = 8
HALVES = 2
NH = N // HALVES
LAST_CUTS = 4
BLOCK3 = (CB - 1) * 2 * F
LATE_VAL = 4
EARLY = BLOCK3 - LATE_VAL * P

FLOPS = 2 * C * (2 * F) * N + 2 * F * C * N


def tile_vanillatransformer_kernel(tc, tok_emb, pos_enc, w_in, w_out, offs, out):
    nc = tc.nc
    tok_blocks = tok_emb.rearrange("(p k) s -> k p s", k=CB)
    out_blocks = out.rearrange("(p k) j -> k p j", k=CB)
    pos_rows = pos_enc.rearrange("(p k) j -> p k j", k=CB)
    w_in_rows = w_in.rearrange("(p k) f -> p (k f)", k=CB)
    w_out_rows = w_out.rearrange("(f p) (q k) -> p f q k", p=P, k=CB)
    with (
        tc.tile_pool(name="held", bufs=1) as held,
        tc.tile_pool(name="work", bufs=HALVES * CB) as work,
        tc.psum_pool(name="psum", bufs=BANKS) as psum,
    ):
        offsets = held.tile([P, N // 16], U16, name="offsets")
        table = [held.tile([P, S], F32, name=f"table{k}") for k in range(CB)]
        pos = held.tile([P, CB, N], F32, name="pos")
        w_in_sb = held.tile([P, CB * 2 * F], BF16, name="w_in_sb")
        w_out_sb = held.tile([P, FB, P, CB], BF16, name="w_out_sb")
        x32 = [held.tile([P, N], F32, name=f"x32_{k}") for k in range(CB)]
        x16 = [held.tile([P, N], BF16, name=f"x16_{k}") for k in range(CB)]
        h = [[held.tile([P, NH], BF16, name=f"h{a}_{f}") for f in range(FB)] for a in range(HALVES)]

        nc.sync.dma_start(table[0][:], tok_blocks[0])
        nc.sync.dma_start(offsets[:], offs)
        nc.gpsimd.memset(pos[:], 0.0)
        nc.sync.dma_start(pos[0:1, :, :], pos_rows[0:1, :, :])
        for k in range(1, CB - 2):
            nc.sync.dma_start(table[k][:], tok_blocks[k])
        nc.sync.dma_start(w_in_sb[:, :EARLY], w_in_rows[:, :EARLY])
        nc.sync.dma_start(table[CB - 2][:], tok_blocks[CB - 2])
        nc.sync.dma_start(table[CB - 1][:], tok_blocks[CB - 1])
        nc.sync.dma_start(w_in_sb[:, EARLY:BLOCK3], w_in_rows[:, EARLY:BLOCK3])
        nc.sync.dma_start(w_in_sb[:, BLOCK3:], w_in_rows[:, BLOCK3:])
        nc.sync.dma_start(w_out_sb[:], w_out_rows)

        gate_val = [
            [psum.tile([P, 2 * NH], F32, name=f"gate_val{a}_{f}", tag="bank") for f in range(FB)]
            for a in range(HALVES)
        ]
        for k in range(CB):
            cuts = LAST_CUTS if k == CB - 1 else 1
            width = N // cuts
            for t in range(cuts):
                cols = slice(t * width, (t + 1) * width)
                nc.vector.tensor_tensor(
                    x32[k][:, cols],
                    table[k][:].indirect(offsets[:, t * width // 16 : (t + 1) * width // 16]),
                    pos[:, k, cols],
                    ADD,
                )
                nc.scalar.activation(x16[k][:, cols], x32[k][:, cols], COPY)
            products = [(a, f, v) for a in range(HALVES) for f in range(FB) for v in range(2)]
            if k == CB - 2:
                products = sorted(products, key=lambda afv: afv[2] == 1 and afv[1] >= FB - LATE_VAL)
            for a, f, v in products:
                col = k * 2 * F + v * F + f * P
                nc.tensor.matmul(
                    gate_val[a][f][:, v * NH : (v + 1) * NH],
                    w_in_sb[:, col : col + P],
                    x16[k][:, a * NH : (a + 1) * NH],
                    start=k == 0 and v == 0,
                    stop=k == CB - 1 and v == 1,
                )

        for a in range(HALVES):
            for f in range(FB):
                relu_gate = work.tile([P, NH], F32, name="relu_gate")
                nc.scalar.activation(relu_gate[:], gate_val[a][f][:, :NH], RELU)
                nc.vector.tensor_tensor(h[a][f][:], relu_gate[:], gate_val[a][f][:, NH:], MULT)

        units = [(a, m, 0, NH) for a in range(HALVES) for m in range(CB)]
        units = units[:-1] + [(HALVES - 1, CB - 1, 0, NH // 2), (HALVES - 1, CB - 1, NH // 2, NH)]
        for a, m, lo, hi in units:
            tokens = slice(a * NH + lo, a * NH + hi)
            ffn = psum.tile([P, NH], F32, name="ffn", tag="bank")
            for f in range(FB):
                nc.tensor.matmul(
                    ffn[:, : hi - lo], w_out_sb[:, f, :, m], h[a][f][:, lo:hi], start=f == 0, stop=f == FB - 1
                )
            result = work.tile([P, NH], F32, name="result")
            nc.vector.tensor_tensor(result[:, : hi - lo], ffn[:, : hi - lo], x32[m][:, tokens], ADD)
            nc.sync.dma_start(out_blocks[m][:, tokens], result[:, : hi - lo])
